import numpy as np
import ml_dtypes


def mxq(x, axis, fmt="e4m3"):
    dtype, down = {"e4m3": (ml_dtypes.float8_e4m3fn, 7), "e5m2": (ml_dtypes.float8_e5m2, 14)}[fmt]
    v = np.moveaxis(np.asarray(x, np.float32).astype(ml_dtypes.bfloat16).astype(np.float64), axis, -1)
    blocks = v.reshape(v.shape[:-1] + (-1, 32))
    amax = np.abs(blocks).max(-1, keepdims=True)
    byte = np.maximum(np.where(amax > 0, np.frexp(amax)[1] - 1 + 127, 0) - down, 1)
    scale = np.exp2(byte - 127.0)
    codes = (blocks / scale).astype(np.float32).astype(dtype).astype(np.float64)
    return np.moveaxis((codes * scale).reshape(v.shape), -1, axis)


WIDE = False


def mx_kscale(k):
    if not WIDE:
        return np.ones(k)
    levels = np.array([10, -10, 5, -5, 0])
    if k % 512:
        return np.exp2(np.random.permutation(np.resize(levels, k // 32))).repeat(32)
    a = np.empty((k // 512, 16))
    for p in range(k // 512):
        a[p, :8] = np.random.permutation(np.resize(levels, 8))
        for g in range(8):
            far = levels[np.abs(levels - a[p, g]) >= 10]
            a[p, g + 8] = far[np.random.randint(len(far))]
    return np.exp2(a.ravel()).repeat(32)


BF16 = ml_dtypes.bfloat16


def bf(x):
    return np.asarray(x, np.float32).astype(BF16)


def f64(x):
    return np.asarray(x).astype(np.float64)


B, N, C_IN, C_OUT, RANK = 2, 2048, 1024, 1024, 128


def sigmoid(v):
    return 1.0 / (1.0 + np.exp(-v))


def setup_inputs():
    s = mx_kscale(C_IN)
    return {"x": bf(np.random.standard_normal((B, N, C_IN)) * s),
            "freq": bf(np.random.standard_normal((B, RANK * (C_IN + C_OUT)))),
            "phase_shift": bf(np.random.standard_normal((B, 2 * C_OUT))),
            "weight": bf(np.random.standard_normal((C_OUT, C_IN)) / np.sqrt(C_IN) / s[None, :])}


def reference(x, freq, phase_shift, weight):
    x, freq, phase_shift, weight = f64(x), f64(freq), f64(phase_shift), f64(weight)
    c_out, c_in = weight.shape
    rank = freq.shape[1] // (c_in + c_out)
    left = freq[:, :c_out * rank].reshape(-1, c_out, rank)
    right = freq[:, c_out * rank:].reshape(-1, rank, c_in)
    modulation = (left @ right) / np.sqrt(rank)
    modulation = sigmoid(modulation) - 0.5
    W = weight[None, :, :] * (modulation + 1.0)
    out = mxq(x, 2, "e4m3") @ mxq(W, 2, "e4m3").transpose(0, 2, 1)
    freq_shift = phase_shift[:, :c_out][:, None, :]
    phase = ((phase_shift[:, c_out:] - 30.0) / 15.0)[:, None, :]
    return np.sin(freq_shift * out + phase)

@@ -1,0 +1,405 @@
+import math
+from contextlib import ExitStack
+
+import concourse.mybir as mybir
+from concourse.masks import make_identity
+
+F32 = mybir.dt.float32
+BF16 = mybir.dt.bfloat16
+I32 = mybir.dt.int32
+U32 = mybir.dt.uint32
+U8 = mybir.dt.uint8
+FP8X4 = mybir.dt.float8_e4m3fn_x4
+ACT = mybir.ActivationFunctionType
+ALU = mybir.AluOpType
+
+P = 128
+B, N, CI, CO, R = 2, 2048, 1024, 1024, 128
+FLOPS = 2 * B * N * CI * CO + 2 * B * CO * CI * R
+ROWS = N // P
+TQ = 4
+NCH = B * (ROWS // TQ)
+NPAIR = NCH * 4
+TWO_PI = 2.0 * math.pi
+
+HEAD = 8
+HEAD_TAGS = ("a", "a", "y", "y", "t", "t")
+D_K, D_R, D_T = 1, 2, 3
+X_LEAD = 7
+U_DVE_FROM = 22
+
+
+def take(queue):
+    items = list(queue)
+    queue[:] = []
+    return items
+
+
+def tile_fmmlayer_t_kernel(tc, x, freq, phase_shift, weight, out):
+    nc = tc.nc
+    with ExitStack() as ctx:
+        keep = ctx.enter_context(tc.tile_pool(name="keep", bufs=1))
+        xs_pool = ctx.enter_context(tc.tile_pool(name="xs", bufs=4))
+        st2 = ctx.enter_context(tc.tile_pool(name="st2", bufs=2))
+        st3 = ctx.enter_context(tc.tile_pool(name="st3", bufs=3))
+        st4 = ctx.enter_context(tc.tile_pool(name="st4", bufs=4))
+        psum = ctx.enter_context(tc.psum_pool(name="psum", bufs=2))
+        ctx.enter_context(tc.manual_schedule())
+
+        ident_b = keep.tile([P, P], BF16, name="ident_b")
+        make_identity(nc, ident_b[:])
+        ident_f = keep.tile([P, P], F32, name="ident_f")
+        make_identity(nc, ident_f[:])
+        warm_in = keep.tile([P, 1], F32, name="warm_in")
+        nc.vector.memset(warm_in[:], 0.0)
+        warm_out = keep.tile([P, 1], F32, name="warm_out")
+        nc.scalar.activation(out=warm_out[:], in_=warm_in[:], func=ACT.Silu)
+
+        psz = keep.tile([P, P], BF16, name="psz")
+        nc.vector.memset(psz[:], 0.0)
+        nc.sync.dma_start(out=psz[0:32, :], in_=phase_shift.rearrange("b (r c) -> (b r) c", c=P))
+        lf = []
+        rt = []
+        wn = []
+        for b in range(B):
+            lf.append(keep.tile([P, 8, R], BF16, name="lf%d" % b))
+            rt.append(keep.tile([P, CI], BF16, name="rt%d" % b))
+        for k in range(4):
+            wn.append(keep.tile([P, 2, CI], BF16, name="wn%d" % k))
+        wview = weight.rearrange("(t p) i -> p t i", p=P)
+
+        def load_freq(b):
+            nc.sync.dma_start(out=lf[b][:], in_=freq[b, 0 : CO * R].rearrange("(t p r) -> p t r", t=8, p=P))
+            nc.sync.dma_start(out=rt[b][:], in_=freq[b, CO * R : CO * R + R * CI].rearrange("(r i) -> r i", r=R))
+
+        def load_w(k):
+            nc.sync.dma_start(out=wn[k][:], in_=wview[:, 2 * k : 2 * k + 2, :])
+
+        xs = {}
+
+        def load_x(c):
+            b, q = divmod(c, 4)
+            xs_t = xs_pool.tile([P, TQ, CI], BF16, name="xs_t", tag="xs")
+            nc.sync.dma_start(
+                out=xs_t[:], in_=x[b].rearrange("(j s) i -> j s i", s=ROWS)[:, TQ * q : TQ * q + TQ, :]
+            )
+            xs[c] = xs_t
+
+        load_freq(0)
+        load_w(0)
+        load_w(1)
+        load_x(0)
+        load_w(2)
+        load_w(3)
+        load_freq(1)
+        load_x(1)
+        load_x(2)
+        load_x(3)
+
+        later_act = []
+        later_dve = []
+        pending = []
+        head = {"on": False, "n": 0}
+
+        def w_bank(shape, dtype):
+            tag = "a"
+            if head["on"]:
+                tag = HEAD_TAGS[head["n"] % len(HEAD_TAGS)]
+                head["n"] += 1
+            wb = psum.tile(shape, dtype, name="wb", tag=tag)
+            return wb
+
+        pps = w_bank([P, P], BF16)
+        nc.tensor.transpose(pps[:], psz[:], ident_b[:])
+        psv = pps[:, 0:32].rearrange("p (b h o) -> p b h o", b=B, h=2)
+        fs2 = keep.tile([P, B, 8], F32, name="fs2")
+        ph2 = keep.tile([P, B, 8], F32, name="ph2")
+        nc.vector.tensor_scalar(out=fs2[:], in0=psv[:, :, 0, :], scalar1=1.0 / TWO_PI, scalar2=None, op0=ALU.mult)
+        nc.vector.tensor_scalar(
+            out=ph2[:], in0=psv[:, :, 1, :], scalar1=-30.0, scalar2=1.0 / (15.0 * TWO_PI), op0=ALU.add, op1=ALU.mult
+        )
+
+        lT = []
+        wc = []
+        wsc = []
+        for b in range(B):
+            lT.append(keep.tile([P, CO], BF16, name="lT%d" % b))
+            wc.append(keep.tile([P, 2, CO], U32, name="wc%d" % b, align_bytes=64))
+            wsc.append(keep.tile([P, 2, CO], U8, name="wsc%d" % b, align_bytes=64))
+        wTh = keep.tile([P, 2, CO, 4], BF16, name="wTh")
+        wThf = wTh[:].bitcast(F32)
+
+        def step_left(b):
+            plf = w_bank([P, 8, P], BF16)
+            for t in range(8):
+                nc.tensor.transpose(plf[:, t, :], lf[b][:, t, :], ident_b[:])
+            later_act.append(lambda: nc.scalar.copy(out=lT[b][:], in_=plf[:].rearrange("p t o -> p (t o)")))
+
+        def step_halve(k):
+            flat = wn[k][:].rearrange("p t i -> p (t i)")
+            nc.vector.tensor_scalar(out=flat, in0=flat, scalar1=0.5, scalar2=None, op0=ALU.mult)
+
+        def step_wt(k, g):
+            wnf = wn[k][:].bitcast(F32)
+            pw = w_bank([P, 2, 256], F32)
+            for u in range(2):
+                for ol in range(2):
+                    nc.tensor.transpose(pw[:, u, ol * P : (ol + 1) * P], wnf[:, ol, 256 * g + u : 256 * (g + 1) : 2], ident_f[:])
+            dst = wThf[:, g, 256 * k : 256 * k + 256, :]
+            src = pw[:].rearrange("p u o -> p o u")
+            later_act.append(lambda: nc.scalar.copy(out=dst, in_=src))
+
+        th_now = {}
+
+        def step_w(b, g, oq, ol):
+            if ol == 0:
+                th_new = st3.tile([P, 256, 4], F32, name="th_new", tag="th")
+                th_now["t"] = th_new
+            th = th_now["t"]
+            ot = 2 * oq + ol
+            rtv = rt[b][:].rearrange("r (g p u e) -> r g u e p", g=2, u=2, p=P, e=2)
+            pm = w_bank([P, 4, P], F32)
+            for u in range(2):
+                for e in range(2):
+                    nc.tensor.matmul(
+                        out=pm[:, 2 * u + e, :],
+                        lhsT=rtv[:, g, u, e, :],
+                        rhs=lT[b][:, ot * P : (ot + 1) * P],
+                        start=True,
+                        stop=True,
+                    )
+
+            def quant(gw):
+                nc.vector.quantize_mx(
+                    out=wc[b][:, g, 256 * oq : 256 * oq + 256].bitcast(FP8X4),
+                    scales=wsc[b][:, g, 256 * oq : 256 * oq + 256],
+                    in_=gw[:].rearrange("p o t -> p (o t)"),
+                )
+
+            def modulate():
+                gw = st2.tile([P, 256, 4], BF16, name="gw", tag="gw", align_bytes=64)
+                nc.vector.scalar_tensor_tensor(
+                    out=gw[:].rearrange("p o t -> p (o t)"),
+                    in0=th[:].rearrange("p o t -> p (o t)"),
+                    scalar=2.0,
+                    in1=wTh[:, g, 256 * oq : 256 * oq + 256, :].rearrange("p o t -> p (o t)"),
+                    op0=ALU.add,
+                    op1=ALU.mult,
+                )
+                pending.append(lambda: quant(gw))
+
+            def tanh():
+                nc.scalar.activation(
+                    out=th[:, ol * P : (ol + 1) * P, :],
+                    in_=pm[:].rearrange("p t o -> p o t"),
+                    func=ACT.Tanh,
+                    scale=0.5 / math.sqrt(R),
+                )
+                if ol == 1:
+                    pending.append(modulate)
+
+            later_act.append(tanh)
+
+        w_steps = []
+
+        def add_w(b, oq):
+            for g in range(2):
+                for ol in range(2):
+                    w_steps.append((True, lambda g=g, ol=ol: step_w(b, g, oq, ol)))
+
+        def add_wt(k):
+            for g in range(2):
+                w_steps.append((True, lambda g=g: step_wt(k, g)))
+
+        w_steps.append((False, lambda: step_halve(0)))
+        w_steps.append((True, lambda: step_left(0)))
+        add_w(0, 0)
+        add_wt(0)
+        w_steps.append((False, lambda: step_halve(1)))
+        for k in range(1, 4):
+            add_wt(k)
+            if k < 3:
+                w_steps.append((False, lambda k=k: step_halve(k + 1)))
+            add_w(0, k)
+        w_steps.append((True, lambda: step_left(1)))
+        for k in range(4):
+            add_w(1, k)
+        w_pos = {"i": 0}
+
+        def w_free():
+            while w_pos["i"] < len(w_steps) and not w_steps[w_pos["i"]][0]:
+                w_steps[w_pos["i"]][1]()
+                w_pos["i"] += 1
+
+        def w_next():
+            w_free()
+            w_steps[w_pos["i"]][1]()
+            w_pos["i"] += 1
+            w_free()
+
+        xc = {}
+        xsc = {}
+        gx = {}
+
+        def x_quant(c, g):
+            nc.vector.quantize_mx(
+                out=xc[c][:, g, :].bitcast(FP8X4),
+                scales=xsc[c][:, g, :],
+                in_=gx[(c, g)][:].rearrange("p n t -> p (n t)"),
+            )
+
+        def step_x(s):
+            c, sub = divmod(s, 4)
+            g, tp = divmod(sub, 2)
+            if sub == 0:
+                xc_t = st3.tile([P, 2, 512], U32, name="xc_t", tag="xc", align_bytes=64)
+                xsc_t = st3.tile([P, 2, 512], U8, name="xsc_t", tag="xsc", align_bytes=64)
+                xc[c] = xc_t
+                xsc[c] = xsc_t
+            if tp == 0:
+                gx_t = st4.tile([P, 512, 4], BF16, name="gx_t", tag="gx", align_bytes=64)
+                gx[(c, g)] = gx_t
+            xf = xs[c][:].bitcast(F32)
+            px = psum.tile([P, 2, 256], F32, name="px", tag="x")
+            for u in range(2):
+                for tl in range(2):
+                    nc.tensor.transpose(px[:, u, tl * P : (tl + 1) * P], xf[:, 2 * tp + tl, 256 * g + u : 256 * (g + 1) : 2], ident_f[:])
+            dst = gx[(c, g)][:].bitcast(F32)[:, 256 * tp : 256 * tp + 256, :]
+            src = px[:].rearrange("p u n -> p n u")
+            if s % 2 == 0:
+                later_act.append(lambda: nc.scalar.copy(out=dst, in_=src))
+            else:
+                later_dve.append(lambda: nc.vector.tensor_copy(out=dst, in_=src))
+            if sub == 3 and c + 4 < NCH:
+                load_x(c + 4)
+            if tp == 1:
+                later_dve.append(lambda: pending.append(lambda: pending.append(lambda: x_quant(c, g))))
+
+        ys = {}
+        us = {}
+        ks = {}
+        rs = {}
+
+        def where(i):
+            c, pr = divmod(i, 4)
+            b, q = divmod(c, 4)
+            return b, q, c, pr
+
+        def s_mx(i):
+            b, q, c, pr = where(i)
+            for ol in range(2):
+                ot = 2 * pr + ol
+                py = psum.tile([P, 512], F32, name="py", tag="y")
+                for g in range(2):
+                    nc.tensor.matmul_mx(
+                        out=py[:],
+                        lhsT=wc[b][:, g, ot * P : (ot + 1) * P].bitcast(FP8X4),
+                        lhsT_scale=wsc[b][:, g, ot * P : (ot + 1) * P],
+                        rhs=xc[c][:, g, :].bitcast(FP8X4),
+                        rhs_scale=xsc[c][:, g, :],
+                        start=(g == 0),
+                        stop=(g == 1),
+                    )
+                ys[(i, ol)] = py
+            u_t = st4.tile([P, 2, 512], F32, name="u_t", tag="u")
+            us[i] = u_t
+
+        def s_u(i, on_dve):
+            b, q, c, pr = where(i)
+            for ol in range(2):
+                ot = 2 * pr + ol
+                if (i >= U_DVE_FROM and i % 2 == 0 and ol == 1) != on_dve:
+                    continue
+                if on_dve:
+                    nc.vector.tensor_scalar(
+                        out=us[i][:, ol, :],
+                        in0=ys[(i, ol)][:],
+                        scalar1=fs2[:, b, ot : ot + 1],
+                        scalar2=ph2[:, b, ot : ot + 1],
+                        op0=ALU.mult,
+                        op1=ALU.add,
+                    )
+                else:
+                    nc.scalar.activation(
+                        out=us[i][:, ol, :],
+                        in_=ys[(i, ol)][:],
+                        func=ACT.Identity,
+                        scale=fs2[:, b, ot : ot + 1],
+                        bias=ph2[:, b, ot : ot + 1],
+                    )
+
+        def s_k(i):
+            k_t = st3.tile([P, 2, 512], I32, name="k_t", tag="k")
+            nc.vector.tensor_copy(out=k_t[:], in_=us[i][:])
+            ks[i] = k_t
+
+        def s_r(i):
+            r_t = st3.tile([P, 2, 512], F32, name="r_t", tag="r")
+            nc.vector.tensor_tensor(out=r_t[:], in0=us[i][:], in1=ks[i][:], op=ALU.subtract)
+            rs[i] = r_t
+
+        def s_out(i):
+            b, q, c, pr = where(i)
+            pts = []
+            for ol in range(2):
+                pt = psum.tile([P, TQ, P], F32, name="pt", tag="t")
+                for t in range(TQ):
+                    nc.tensor.transpose(pt[:, t, :], rs[i][:, ol, t * P : (t + 1) * P], ident_f[:])
+                pts.append(pt)
+            ob = st3.tile([P, TQ, 2 * P], F32, name="ob", tag="ob")
+            oview = out[b].rearrange("(j s) o -> j s o", s=ROWS)[:, TQ * q : TQ * q + TQ, :]
+            for ol in range(2):
+                nc.scalar.activation(out=ob[:, :, ol * P : (ol + 1) * P], in_=pts[ol][:], func=ACT.Sin, scale=TWO_PI)
+                if i == NPAIR - 1:
+                    o0 = (2 * pr + ol) * P
+                    nc.sync.dma_start(out=oview[:, :, o0 : o0 + P], in_=ob[:, :, ol * P : (ol + 1) * P])
+            if i < NPAIR - 1:
+                nc.sync.dma_start(out=oview[:, :, 2 * pr * P : (2 * pr + 2) * P], in_=ob[:])
+
+        def n_w(i):
+            if i == -HEAD or i == -1:
+                return 1
+            if i == 1 - HEAD:
+                return 6
+            if i == -2:
+                return 2
+            if i < -1:
+                return 4
+            if i < 16:
+                return 1
+            return 0
+
+        def n_x(i):
+            if i == 2 - HEAD or i == 3 - HEAD:
+                return 2
+            if 4 - X_LEAD <= i < 4 * NCH - X_LEAD:
+                return 1
+            return 0
+
+        x_pos = {"s": 0}
+        for i in range(-HEAD, NPAIR + D_T):
+            head["on"] = i < -1
+            if 0 <= i < NPAIR:
+                s_mx(i)
+            for f in take(later_act):
+                f()
+            if 0 <= i < NPAIR:
+                s_u(i, False)
+            if 0 <= i - D_K < NPAIR:
+                s_k(i - D_K)
+            if 0 <= i - D_R < NPAIR:
+                s_r(i - D_R)
+            if 0 <= i < NPAIR:
+                s_u(i, True)
+            for f in take(later_dve):
+                f()
+            for f in take(pending):
+                f()
+            if 0 <= i - D_T < NPAIR:
+                s_out(i - D_T)
+            for j in range(max(n_w(i), n_x(i))):
+                if j < n_w(i):
+                    w_next()
+                if j < n_x(i):
+                    step_x(x_pos["s"])
+                    x_pos["s"] += 1

@@ -22,11 +22,13 @@ NCH = B * (ROWS // TQ)
 NPAIR = NCH * 4
 TWO_PI = 2.0 * math.pi
 
-HEAD = 8
-HEAD_TAGS = ("a", "a", "y", "y", "t", "t")
 D_K, D_R, D_T = 1, 2, 3
-X_LEAD = 7
-U_DVE_FROM = 22
+W_END = 20
+X_END = 28
+U_DVE_FROM = 28
+U_MOD = 2
+X_DVE_A = 20
+HALF_LAST = 2
 
 
 def take(queue):
@@ -40,24 +42,22 @@ def tile_fmmlayer_t_kernel(tc, x, freq, phase_shift, weight, out):
     with ExitStack() as ctx:
         keep = ctx.enter_context(tc.tile_pool(name="keep", bufs=1))
         xs_pool = ctx.enter_context(tc.tile_pool(name="xs", bufs=4))
-        st2 = ctx.enter_context(tc.tile_pool(name="st2", bufs=2))
         st3 = ctx.enter_context(tc.tile_pool(name="st3", bufs=3))
         st4 = ctx.enter_context(tc.tile_pool(name="st4", bufs=4))
-        psum = ctx.enter_context(tc.psum_pool(name="psum", bufs=2))
+        psum = ctx.enter_context(tc.psum_pool(name="psum", bufs=1))
         ctx.enter_context(tc.manual_schedule())
 
         ident_b = keep.tile([P, P], BF16, name="ident_b")
         make_identity(nc, ident_b[:])
         ident_f = keep.tile([P, P], F32, name="ident_f")
         make_identity(nc, ident_f[:])
+        psz = keep.tile([P, P], BF16, name="psz")
+        nc.vector.memset(psz[:], 0.0)
         warm_in = keep.tile([P, 1], F32, name="warm_in")
         nc.vector.memset(warm_in[:], 0.0)
         warm_out = keep.tile([P, 1], F32, name="warm_out")
         nc.scalar.activation(out=warm_out[:], in_=warm_in[:], func=ACT.Silu)
 
-        psz = keep.tile([P, P], BF16, name="psz")
-        nc.vector.memset(psz[:], 0.0)
-        nc.sync.dma_start(out=psz[0:32, :], in_=phase_shift.rearrange("b (r c) -> (b r) c", c=P))
         lf = []
         rt = []
         wn = []
@@ -65,59 +65,93 @@ def tile_fmmlayer_t_kernel(tc, x, freq, phase_shift, weight, out):
             lf.append(keep.tile([P, 8, R], BF16, name="lf%d" % b))
             rt.append(keep.tile([P, CI], BF16, name="rt%d" % b))
         for k in range(4):
-            wn.append(keep.tile([P, 2, CI], BF16, name="wn%d" % k))
+            wn.append([keep.tile([P, 2, CI // 2], BF16, name="wn%d_%d" % (k, g)) for g in range(2)])
         wview = weight.rearrange("(t p) i -> p t i", p=P)
 
-        def load_freq(b):
-            nc.sync.dma_start(out=lf[b][:], in_=freq[b, 0 : CO * R].rearrange("(t p r) -> p t r", t=8, p=P))
-            nc.sync.dma_start(out=rt[b][:], in_=freq[b, CO * R : CO * R + R * CI].rearrange("(r i) -> r i", r=R))
+        def load_left(b, t0, t1):
+            nc.sync.dma_start(
+                out=lf[b][:, t0:t1, :],
+                in_=freq[b, t0 * P * R : t1 * P * R].rearrange("(t p r) -> p t r", t=t1 - t0, p=P),
+            )
 
-        def load_w(k):
-            nc.sync.dma_start(out=wn[k][:], in_=wview[:, 2 * k : 2 * k + 2, :])
+        def load_right(b, g=None):
+            i0, i1 = (0, CI) if g is None else (512 * g, 512 * g + 512)
+            nc.sync.dma_start(
+                out=rt[b][:, i0:i1], in_=freq[b, CO * R : CO * R + R * CI].rearrange("(r i) -> r i", r=R)[:, i0:i1]
+            )
+
+        def load_w(k, g):
+            nc.sync.dma_start(out=wn[k][g][:], in_=wview[:, 2 * k : 2 * k + 2, 512 * g : 512 * (g + 1)])
 
         xs = {}
 
-        def load_x(c):
+        def load_x(c, parts=1):
             b, q = divmod(c, 4)
             xs_t = xs_pool.tile([P, TQ, CI], BF16, name="xs_t", tag="xs")
-            nc.sync.dma_start(
-                out=xs_t[:], in_=x[b].rearrange("(j s) i -> j s i", s=ROWS)[:, TQ * q : TQ * q + TQ, :]
-            )
+            w = TQ // parts
+            for h in range(parts):
+                t0 = TQ * q + w * h
+                nc.sync.dma_start(
+                    out=xs_t[:, w * h : w * h + w, :],
+                    in_=x[b].rearrange("(j s) i -> j s i", s=ROWS)[:, t0 : t0 + w, :],
+                )
             xs[c] = xs_t
 
-        load_freq(0)
-        load_w(0)
-        load_w(1)
-        load_x(0)
-        load_w(2)
-        load_w(3)
-        load_freq(1)
+        load_left(0, 0, 4)
+        load_right(0, 0)
+        load_w(0, 0)
+        load_right(0, 1)
+        load_w(0, 1)
+        load_left(0, 4, 8)
+        load_w(1, 0)
+        load_w(1, 1)
+        load_x(0, 2)
+        load_w(2, 0)
+        load_w(2, 1)
+        nc.sync.dma_start(out=psz[0:32, :], in_=phase_shift.rearrange("b (r c) -> (b r) c", c=P))
+        load_w(3, 0)
+        load_w(3, 1)
         load_x(1)
+        load_left(1, 0, 8)
+        load_right(1)
         load_x(2)
         load_x(3)
 
-        later_act = []
-        later_dve = []
-        pending = []
-        head = {"on": False, "n": 0}
+        turn = {"head": 0, "y": 0, "t": 0, "w": 0, "x": 0}
 
-        def w_bank(shape, dtype):
-            tag = "a"
-            if head["on"]:
-                tag = HEAD_TAGS[head["n"] % len(HEAD_TAGS)]
-                head["n"] += 1
-            wb = psum.tile(shape, dtype, name="wb", tag=tag)
-            return wb
+        def bank(role, i, shape, dtype):
+            if i < 0:
+                banks, role = (0, 1, 2, 3, 4, 5, 6, 7), "head"
+            elif role == "y":
+                banks = (0, 1, 4, 5) if i >= W_END else (0, 1)
+            elif role == "t":
+                banks = (2, 3, 6, 7) if i >= X_END else (2, 3)
+            elif role == "w":
+                banks = (4, 5)
+            else:
+                banks = (6, 7)
+            n = turn[role]
+            turn[role] += 1
+            ps = psum.tile(shape, dtype, name="ps", tag="bank%d" % banks[n % len(banks)])
+            return ps
 
-        pps = w_bank([P, P], BF16)
-        nc.tensor.transpose(pps[:], psz[:], ident_b[:])
-        psv = pps[:, 0:32].rearrange("p (b h o) -> p b h o", b=B, h=2)
         fs2 = keep.tile([P, B, 8], F32, name="fs2")
         ph2 = keep.tile([P, B, 8], F32, name="ph2")
-        nc.vector.tensor_scalar(out=fs2[:], in0=psv[:, :, 0, :], scalar1=1.0 / TWO_PI, scalar2=None, op0=ALU.mult)
-        nc.vector.tensor_scalar(
-            out=ph2[:], in0=psv[:, :, 1, :], scalar1=-30.0, scalar2=1.0 / (15.0 * TWO_PI), op0=ALU.add, op1=ALU.mult
-        )
+
+        def phase(i):
+            pps = bank("x", i, [P, P], BF16)
+            nc.tensor.transpose(pps[:], psz[:], ident_b[:])
+
+            def leave():
+                psv = pps[:, 0:32].rearrange("p (b h o) -> p b h o", b=B, h=2)
+                nc.vector.tensor_scalar(
+                    out=fs2[:], in0=psv[:, :, 0, :], scalar1=0.5 / TWO_PI, scalar2=None, op0=ALU.mult
+                )
+                nc.vector.tensor_scalar(
+                    out=ph2[:], in0=psv[:, :, 1, :], scalar1=-30.0, scalar2=1.0 / (15.0 * TWO_PI), op0=ALU.add, op1=ALU.mult
+                )
+
+            return leave
 
         lT = []
         wc = []
@@ -129,36 +163,38 @@ def tile_fmmlayer_t_kernel(tc, x, freq, phase_shift, weight, out):
         wTh = keep.tile([P, 2, CO, 4], BF16, name="wTh")
         wThf = wTh[:].bitcast(F32)
 
-        def step_left(b):
-            plf = w_bank([P, 8, P], BF16)
-            for t in range(8):
-                nc.tensor.transpose(plf[:, t, :], lf[b][:, t, :], ident_b[:])
-            later_act.append(lambda: nc.scalar.copy(out=lT[b][:], in_=plf[:].rearrange("p t o -> p (t o)")))
+        def copy_on(engine, dst, src):
+            if engine == "v":
+                nc.vector.tensor_copy(out=dst, in_=src)
+            else:
+                nc.scalar.copy(out=dst, in_=src)
 
-        def step_halve(k):
-            flat = wn[k][:].rearrange("p t i -> p (t i)")
-            nc.vector.tensor_scalar(out=flat, in0=flat, scalar1=0.5, scalar2=None, op0=ALU.mult)
+        def left(b, t0, t1, i):
+            plf = bank("x", i, [P, 8, P], BF16)
+            for t in range(t0, t1):
+                nc.tensor.transpose(plf[:, t - t0, :], lf[b][:, t, :], ident_b[:])
+            return lambda e: copy_on(
+                e, lT[b][:, t0 * P : t1 * P], plf[:, 0 : t1 - t0, :].rearrange("p t o -> p (t o)")
+            )
 
-        def step_wt(k, g):
-            wnf = wn[k][:].bitcast(F32)
-            pw = w_bank([P, 2, 256], F32)
+        def wt(k, g, i):
+            wnf = wn[k][g][:].bitcast(F32)
+            pw = bank("t", i, [P, 2, 256], F32)
             for u in range(2):
                 for ol in range(2):
-                    nc.tensor.transpose(pw[:, u, ol * P : (ol + 1) * P], wnf[:, ol, 256 * g + u : 256 * (g + 1) : 2], ident_f[:])
-            dst = wThf[:, g, 256 * k : 256 * k + 256, :]
-            src = pw[:].rearrange("p u o -> p o u")
-            later_act.append(lambda: nc.scalar.copy(out=dst, in_=src))
+                    nc.tensor.transpose(pw[:, u, ol * P : (ol + 1) * P], wnf[:, ol, u:256:2], ident_f[:])
+            return lambda e: copy_on(e, wThf[:, g, 256 * k : 256 * k + 256, :], pw[:].rearrange("p u o -> p o u"))
 
-        th_now = {}
+        ths = {}
+        gws = {}
 
-        def step_w(b, g, oq, ol):
+        def wmm(b, oq, g, ol, i):
             if ol == 0:
-                th_new = st3.tile([P, 256, 4], F32, name="th_new", tag="th")
-                th_now["t"] = th_new
-            th = th_now["t"]
+                th = st3.tile([P, 256, 4], F32, name="th", tag="th")
+                ths[(b, oq, g)] = th
             ot = 2 * oq + ol
             rtv = rt[b][:].rearrange("r (g p u e) -> r g u e p", g=2, u=2, p=P, e=2)
-            pm = w_bank([P, 4, P], F32)
+            pm = bank("w", i, [P, 4, P], F32)
             for u in range(2):
                 for e in range(2):
                     nc.tensor.matmul(
@@ -168,89 +204,46 @@ def tile_fmmlayer_t_kernel(tc, x, freq, phase_shift, weight, out):
                         start=True,
                         stop=True,
                     )
+            return lambda: nc.scalar.activation(
+                out=ths[(b, oq, g)][:, ol * P : (ol + 1) * P, :],
+                in_=pm[:].rearrange("p t o -> p o t"),
+                func=ACT.Tanh,
+                scale=0.5 / math.sqrt(R),
+            )
 
-            def quant(gw):
-                nc.vector.quantize_mx(
-                    out=wc[b][:, g, 256 * oq : 256 * oq + 256].bitcast(FP8X4),
-                    scales=wsc[b][:, g, 256 * oq : 256 * oq + 256],
-                    in_=gw[:].rearrange("p o t -> p (o t)"),
-                )
+        def mod(b, oq, g):
+            gw = st3.tile([P, 256, 4], BF16, name="gw", tag="gw", align_bytes=64)
+            gws[(b, oq, g)] = gw
+            nc.vector.scalar_tensor_tensor(
+                out=gw[:].rearrange("p o t -> p (o t)"),
+                in0=ths[(b, oq, g)][:].rearrange("p o t -> p (o t)"),
+                scalar=2.0,
+                in1=wTh[:, g, 256 * oq : 256 * oq + 256, :].rearrange("p o t -> p (o t)"),
+                op0=ALU.add,
+                op1=ALU.mult,
+            )
 
-            def modulate():
-                gw = st2.tile([P, 256, 4], BF16, name="gw", tag="gw", align_bytes=64)
-                nc.vector.scalar_tensor_tensor(
-                    out=gw[:].rearrange("p o t -> p (o t)"),
-                    in0=th[:].rearrange("p o t -> p (o t)"),
-                    scalar=2.0,
-                    in1=wTh[:, g, 256 * oq : 256 * oq + 256, :].rearrange("p o t -> p (o t)"),
-                    op0=ALU.add,
-                    op1=ALU.mult,
-                )
-                pending.append(lambda: quant(gw))
-
-            def tanh():
-                nc.scalar.activation(
-                    out=th[:, ol * P : (ol + 1) * P, :],
-                    in_=pm[:].rearrange("p t o -> p o t"),
-                    func=ACT.Tanh,
-                    scale=0.5 / math.sqrt(R),
-                )
-                if ol == 1:
-                    pending.append(modulate)
-
-            later_act.append(tanh)
-
-        w_steps = []
-
-        def add_w(b, oq):
-            for g in range(2):
-                for ol in range(2):
-                    w_steps.append((True, lambda g=g, ol=ol: step_w(b, g, oq, ol)))
-
-        def add_wt(k):
-            for g in range(2):
-                w_steps.append((True, lambda g=g: step_wt(k, g)))
-
-        w_steps.append((False, lambda: step_halve(0)))
-        w_steps.append((True, lambda: step_left(0)))
-        add_w(0, 0)
-        add_wt(0)
-        w_steps.append((False, lambda: step_halve(1)))
-        for k in range(1, 4):
-            add_wt(k)
-            if k < 3:
-                w_steps.append((False, lambda k=k: step_halve(k + 1)))
-            add_w(0, k)
-        w_steps.append((True, lambda: step_left(1)))
-        for k in range(4):
-            add_w(1, k)
-        w_pos = {"i": 0}
-
-        def w_free():
-            while w_pos["i"] < len(w_steps) and not w_steps[w_pos["i"]][0]:
-                w_steps[w_pos["i"]][1]()
-                w_pos["i"] += 1
-
-        def w_next():
-            w_free()
-            w_steps[w_pos["i"]][1]()
-            w_pos["i"] += 1
-            w_free()
+        def wq(b, oq, g):
+            nc.vector.quantize_mx(
+                out=wc[b][:, g, 256 * oq : 256 * oq + 256].bitcast(FP8X4),
+                scales=wsc[b][:, g, 256 * oq : 256 * oq + 256],
+                in_=gws[(b, oq, g)][:].rearrange("p o t -> p (o t)"),
+            )
 
         xc = {}
         xsc = {}
         gx = {}
 
-        def x_quant(c, g):
+        def xq(c, g):
             nc.vector.quantize_mx(
                 out=xc[c][:, g, :].bitcast(FP8X4),
                 scales=xsc[c][:, g, :],
                 in_=gx[(c, g)][:].rearrange("p n t -> p (n t)"),
             )
 
-        def step_x(s):
+        def xT(s, i):
             c, sub = divmod(s, 4)
-            g, tp = divmod(sub, 2)
+            tp, g = divmod(sub, 2)
             if sub == 0:
                 xc_t = st3.tile([P, 2, 512], U32, name="xc_t", tag="xc", align_bytes=64)
                 xsc_t = st3.tile([P, 2, 512], U8, name="xsc_t", tag="xsc", align_bytes=64)
@@ -260,20 +253,19 @@ def tile_fmmlayer_t_kernel(tc, x, freq, phase_shift, weight, out):
                 gx_t = st4.tile([P, 512, 4], BF16, name="gx_t", tag="gx", align_bytes=64)
                 gx[(c, g)] = gx_t
             xf = xs[c][:].bitcast(F32)
-            px = psum.tile([P, 2, 256], F32, name="px", tag="x")
+            px = bank("x", i, [P, 2, 256], F32)
             for u in range(2):
                 for tl in range(2):
-                    nc.tensor.transpose(px[:, u, tl * P : (tl + 1) * P], xf[:, 2 * tp + tl, 256 * g + u : 256 * (g + 1) : 2], ident_f[:])
-            dst = gx[(c, g)][:].bitcast(F32)[:, 256 * tp : 256 * tp + 256, :]
-            src = px[:].rearrange("p u n -> p n u")
-            if s % 2 == 0:
-                later_act.append(lambda: nc.scalar.copy(out=dst, in_=src))
-            else:
-                later_dve.append(lambda: nc.vector.tensor_copy(out=dst, in_=src))
+                    nc.tensor.transpose(
+                        px[:, u, tl * P : (tl + 1) * P],
+                        xf[:, 2 * tp + tl, 256 * g + u : 256 * (g + 1) : 2],
+                        ident_f[:],
+                    )
             if sub == 3 and c + 4 < NCH:
                 load_x(c + 4)
-            if tp == 1:
-                later_dve.append(lambda: pending.append(lambda: pending.append(lambda: x_quant(c, g))))
+            dst = gx[(c, g)][:].bitcast(F32)[:, 256 * tp : 256 * tp + 256, :]
+            src = px[:].rearrange("p u n -> p n u")
+            return lambda e: copy_on(e, dst, src)
 
         ys = {}
         us = {}
@@ -289,7 +281,7 @@ def tile_fmmlayer_t_kernel(tc, x, freq, phase_shift, weight, out):
             b, q, c, pr = where(i)
             for ol in range(2):
                 ot = 2 * pr + ol
-                py = psum.tile([P, 512], F32, name="py", tag="y")
+                py = bank("y", i, [P, 512], F32)
                 for g in range(2):
                     nc.tensor.matmul_mx(
                         out=py[:],
@@ -308,7 +300,7 @@ def tile_fmmlayer_t_kernel(tc, x, freq, phase_shift, weight, out):
             b, q, c, pr = where(i)
             for ol in range(2):
                 ot = 2 * pr + ol
-                if (i >= U_DVE_FROM and i % 2 == 0 and ol == 1) != on_dve:
+                if (i >= U_DVE_FROM and i % U_MOD == 0 and ol == 1) != on_dve:
                     continue
                 if on_dve:
                     nc.vector.tensor_scalar(
@@ -328,25 +320,30 @@ def tile_fmmlayer_t_kernel(tc, x, freq, phase_shift, weight, out):
                         bias=ph2[:, b, ot : ot + 1],
                     )
 
+        def halves(i):
+            return [slice(0, 1), slice(1, 2)] if i >= NPAIR - HALF_LAST else [slice(0, 2)]
+
         def s_k(i):
             k_t = st3.tile([P, 2, 512], I32, name="k_t", tag="k")
-            nc.vector.tensor_copy(out=k_t[:], in_=us[i][:])
             ks[i] = k_t
+            for h in halves(i):
+                nc.vector.tensor_copy(out=k_t[:, h, :], in_=us[i][:, h, :])
 
         def s_r(i):
             r_t = st3.tile([P, 2, 512], F32, name="r_t", tag="r")
-            nc.vector.tensor_tensor(out=r_t[:], in0=us[i][:], in1=ks[i][:], op=ALU.subtract)
             rs[i] = r_t
+            for h in halves(i):
+                nc.vector.tensor_tensor(out=r_t[:, h, :], in0=us[i][:, h, :], in1=ks[i][:, h, :], op=ALU.subtract)
 
-        def s_out(i):
+        def s_out(i, j):
             b, q, c, pr = where(i)
             pts = []
             for ol in range(2):
-                pt = psum.tile([P, TQ, P], F32, name="pt", tag="t")
+                pt = bank("t", j, [P, TQ, P], F32)
                 for t in range(TQ):
                     nc.tensor.transpose(pt[:, t, :], rs[i][:, ol, t * P : (t + 1) * P], ident_f[:])
                 pts.append(pt)
-            ob = st3.tile([P, TQ, 2 * P], F32, name="ob", tag="ob")
+            ob = st4.tile([P, TQ, 2 * P], F32, name="ob", tag="ob")
             oview = out[b].rearrange("(j s) o -> j s o", s=ROWS)[:, TQ * q : TQ * q + TQ, :]
             for ol in range(2):
                 nc.scalar.activation(out=ob[:, :, ol * P : (ol + 1) * P], in_=pts[ol][:], func=ACT.Sin, scale=TWO_PI)
@@ -356,50 +353,121 @@ def tile_fmmlayer_t_kernel(tc, x, freq, phase_shift, weight, out):
             if i < NPAIR - 1:
                 nc.sync.dma_start(out=oview[:, :, 2 * pr * P : (2 * pr + 2) * P], in_=ob[:])
 
-        def n_w(i):
-            if i == -HEAD or i == -1:
-                return 1
-            if i == 1 - HEAD:
-                return 6
-            if i == -2:
-                return 2
-            if i < -1:
-                return 4
-            if i < 16:
-                return 1
-            return 0
+        H = -1
+        left(0, 0, 4, H)("s")
+        e00 = wt(0, 0, H)
+        e00("v")
+        a = [wmm(0, 0, 0, ol, H) for ol in range(2)]
+        e01 = wt(0, 1, H)
+        e01("v")
+        a += [wmm(0, 0, 1, ol, H) for ol in range(2)]
+        for f in a:
+            f()
+        mod(0, 0, 0)
+        a = [wmm(0, 1, g, ol, H) for g in range(2) for ol in range(2)]
+        mod(0, 0, 1)
+        lb = left(0, 4, 8, H)
+        for f in a:
+            f()
+        lb("s")
+        e10 = wt(1, 0, H)
+        e10("v")
+        e11 = wt(1, 1, H)
+        e11("v")
+        wq(0, 0, 0)
+        wq(0, 0, 1)
+        for s in range(4):
+            ex = xT(s, H)
+            ex("s")
+        mod(0, 1, 0)
+        a = [wmm(0, 2, 0, ol, H) for ol in range(2)]
+        for f in a:
+            f()
+        mod(0, 1, 1)
+        a = [wmm(0, 2, 1, ol, H) for ol in range(2)]
+        for f in a:
+            f()
+        xq(0, 0)
+        xq(0, 1)
+        ph = phase(H)
+        ph()
+        wq(0, 1, 0)
+        wq(0, 1, 1)
+        e20 = wt(2, 0, H)
+        e20("s")
+        e21 = wt(2, 1, H)
+        e21("s")
 
-        def n_x(i):
-            if i == 2 - HEAD or i == 3 - HEAD:
-                return 2
-            if 4 - X_LEAD <= i < 4 * NCH - X_LEAD:
-                return 1
-            return 0
+        later_act = []
+        later_dve = []
+        pend = []
+        x_pos = {"s": 4}
 
-        x_pos = {"s": 0}
-        for i in range(-HEAD, NPAIR + D_T):
-            head["on"] = i < -1
-            if 0 <= i < NPAIR:
+        def w_unit(b, oq, g, ol, i):
+            f = wmm(b, oq, g, ol, i)
+
+            def go():
+                f()
+                if ol == 1:
+                    pend.append(lambda: (mod(b, oq, g), pend.append(lambda: wq(b, oq, g))))
+
+            later_act.append(go)
+
+        def x_unit(i):
+            s = x_pos["s"]
+            if s >= 4 * NCH:
+                return
+            x_pos["s"] += 1
+            c, sub = divmod(s, 4)
+            ex = xT(s, i)
+            if i < X_DVE_A and s % 2 == 0:
+                later_act.append(lambda: ex("s"))
+            else:
+                later_dve.append(lambda: ex("v"))
+            if sub >= 2:
+                later_dve.append(lambda: pend.append(lambda: xq(c, sub % 2)))
+
+        pend.append(lambda: (mod(0, 2, 0), pend.append(lambda: wq(0, 2, 0))))
+        pend.append(lambda: (mod(0, 2, 1), pend.append(lambda: wq(0, 2, 1))))
+        for g in range(2):
+            e3 = wt(3, g, 0)
+            later_dve.append(lambda e3=e3: e3("v"))
+        for ol in range(2):
+            w_unit(0, 3, 0, ol, 0)
+        w_list = []
+        for oq in range(4):
+            for g in range(2):
+                for ol in range(2):
+                    w_list.append(lambda i, oq=oq, g=g, ol=ol: w_unit(1, oq, g, ol, i))
+
+        for i in range(NPAIR + D_T):
+            if i < NPAIR:
                 s_mx(i)
             for f in take(later_act):
                 f()
-            if 0 <= i < NPAIR:
+            if i < NPAIR:
                 s_u(i, False)
             if 0 <= i - D_K < NPAIR:
                 s_k(i - D_K)
             if 0 <= i - D_R < NPAIR:
                 s_r(i - D_R)
-            if 0 <= i < NPAIR:
+            if i < NPAIR:
                 s_u(i, True)
             for f in take(later_dve):
                 f()
-            for f in take(pending):
+            for f in take(pend):
                 f()
             if 0 <= i - D_T < NPAIR:
-                s_out(i - D_T)
-            for j in range(max(n_w(i), n_x(i))):
-                if j < n_w(i):
-                    w_next()
-                if j < n_x(i):
-                    step_x(x_pos["s"])
-                    x_pos["s"] += 1
+                s_out(i - D_T, i)
+            if i == 0:
+                for ol in range(2):
+                    w_unit(0, 3, 1, ol, i)
+                lf1 = left(1, 0, 8, i)
+                later_act.append(lambda: lf1("s"))
+                x_unit(i)
+            elif i <= 16:
+                w_list[i - 1](i)
+            if i in (1, 2):
+                x_unit(i)
+            if i > 0:
+                x_unit(i)

@@ -401,6 +401,7 @@ def tile_fmmlayer_t_kernel(tc, x, freq, phase_shift, weight, out):
         later_act = []
         later_dve = []
         pend = []
+        xqs = []
         x_pos = {"s": 4}
 
         def w_unit(b, oq, g, ol, i):
@@ -425,7 +426,10 @@ def tile_fmmlayer_t_kernel(tc, x, freq, phase_shift, weight, out):
             else:
                 later_dve.append(lambda: ex("v"))
             if sub >= 2:
-                later_dve.append(lambda: pend.append(lambda: xq(c, sub % 2)))
+                if i < W_END:
+                    later_dve.append(lambda: pend.append(lambda: xq(c, sub % 2)))
+                else:
+                    later_dve.append(lambda: xqs.append(lambda: xq(c, sub % 2)))
 
         pend.append(lambda: (mod(0, 2, 0), pend.append(lambda: wq(0, 2, 0))))
         pend.append(lambda: (mod(0, 2, 1), pend.append(lambda: wq(0, 2, 1))))
@@ -447,6 +451,8 @@ def tile_fmmlayer_t_kernel(tc, x, freq, phase_shift, weight, out):
                 f()
             if i < NPAIR:
                 s_u(i, False)
+            for f in take(xqs):
+                f()
             if 0 <= i - D_K < NPAIR:
                 s_k(i - D_K)
             if 0 <= i - D_R < NPAIR:

@@ -24,11 +24,14 @@ TWO_PI = 2.0 * math.pi
 
 D_K, D_R, D_T = 1, 2, 3
 W_END = 20
-X_END = 28
-U_DVE_FROM = 28
+X_END = 20
+U_DVE_FROM = 20
 U_MOD = 2
 X_DVE_A = 20
 HALF_LAST = 2
+X_MOD = 2
+W0 = 8
+X_S_TO = 3
 
 
 def take(queue):
@@ -53,6 +56,8 @@ def tile_fmmlayer_t_kernel(tc, x, freq, phase_shift, weight, out):
         make_identity(nc, ident_f[:])
         psz = keep.tile([P, P], BF16, name="psz")
         nc.vector.memset(psz[:], 0.0)
+        pe_in = keep.tile([P, 512], BF16, name="pe_in")
+        nc.vector.memset(pe_in[:], 0.0)
         warm_in = keep.tile([P, 1], F32, name="warm_in")
         nc.vector.memset(warm_in[:], 0.0)
         warm_out = keep.tile([P, 1], F32, name="warm_out")
@@ -245,8 +250,8 @@ def tile_fmmlayer_t_kernel(tc, x, freq, phase_shift, weight, out):
             c, sub = divmod(s, 4)
             tp, g = divmod(sub, 2)
             if sub == 0:
-                xc_t = st3.tile([P, 2, 512], U32, name="xc_t", tag="xc", align_bytes=64)
-                xsc_t = st3.tile([P, 2, 512], U8, name="xsc_t", tag="xsc", align_bytes=64)
+                xc_t = st3.tile([P, 2, 512], U32, name="xc_t", tag="xc", bufs=5, align_bytes=64)
+                xsc_t = st3.tile([P, 2, 512], U8, name="xsc_t", tag="xsc", bufs=5, align_bytes=64)
                 xc[c] = xc_t
                 xsc[c] = xsc_t
             if tp == 0:
@@ -353,7 +358,13 @@ def tile_fmmlayer_t_kernel(tc, x, freq, phase_shift, weight, out):
             if i < NPAIR - 1:
                 nc.sync.dma_start(out=oview[:, :, 2 * pr * P : (2 * pr + 2) * P], in_=ob[:])
 
+        def warm_pe(n, i):
+            wp = bank("x", i, [P, 512], F32)
+            for m in range(n):
+                nc.tensor.matmul(out=wp[:], lhsT=pe_in[:, 0:P], rhs=pe_in[:], start=True, stop=True)
+
         H = -1
+        warm_pe(W0, H)
         left(0, 0, 4, H)("s")
         e00 = wt(0, 0, H)
         e00("v")
@@ -421,7 +432,7 @@ def tile_fmmlayer_t_kernel(tc, x, freq, phase_shift, weight, out):
             x_pos["s"] += 1
             c, sub = divmod(s, 4)
             ex = xT(s, i)
-            if i < X_DVE_A and s % 2 == 0:
+            if i < X_S_TO or (i < X_DVE_A and s % X_MOD == 0):
                 later_act.append(lambda: ex("s"))
             else:
                 later_dve.append(lambda: ex("v"))
@@ -473,7 +484,7 @@ def tile_fmmlayer_t_kernel(tc, x, freq, phase_shift, weight, out):
                 x_unit(i)
             elif i <= 16:
                 w_list[i - 1](i)
-            if i in (1, 2):
+            if i in (1, 2) or (i % 2 == 0 and 4 <= i < 18):
                 x_unit(i)
             if i > 0:
                 x_unit(i)

@@ -29,8 +29,11 @@ U_DVE_FROM = 20
 U_MOD = 2
 X_DVE_A = 20
 HALF_LAST = 2
+ORDER1 = "oxw"
+ORDER2 = "oxwx"
+XE = 2
+CU = 30
 X_MOD = 2
-W0 = 8
 X_S_TO = 3
 
 
@@ -102,9 +105,10 @@ def tile_fmmlayer_t_kernel(tc, x, freq, phase_shift, weight, out):
                 )
             xs[c] = xs_t
 
-        load_left(0, 0, 4)
+        load_left(0, 0, 2)
         load_right(0, 0)
         load_w(0, 0)
+        load_left(0, 2, 4)
         load_right(0, 1)
         load_w(0, 1)
         load_left(0, 4, 8)
@@ -351,10 +355,14 @@ def tile_fmmlayer_t_kernel(tc, x, freq, phase_shift, weight, out):
             ob = st4.tile([P, TQ, 2 * P], F32, name="ob", tag="ob")
             oview = out[b].rearrange("(j s) o -> j s o", s=ROWS)[:, TQ * q : TQ * q + TQ, :]
             for ol in range(2):
-                nc.scalar.activation(out=ob[:, :, ol * P : (ol + 1) * P], in_=pts[ol][:], func=ACT.Sin, scale=TWO_PI)
-                if i == NPAIR - 1:
-                    o0 = (2 * pr + ol) * P
-                    nc.sync.dma_start(out=oview[:, :, o0 : o0 + P], in_=ob[:, :, ol * P : (ol + 1) * P])
+                cuts = [slice(0, 2), slice(2, 4)] if i == NPAIR - 1 else [slice(0, 4)]
+                for ts in cuts:
+                    nc.scalar.activation(
+                        out=ob[:, ts, ol * P : (ol + 1) * P], in_=pts[ol][:, ts, :], func=ACT.Sin, scale=TWO_PI
+                    )
+                    if i == NPAIR - 1:
+                        o0 = (2 * pr + ol) * P
+                        nc.sync.dma_start(out=oview[:, ts, o0 : o0 + P], in_=ob[:, ts, ol * P : (ol + 1) * P])
             if i < NPAIR - 1:
                 nc.sync.dma_start(out=oview[:, :, 2 * pr * P : (2 * pr + 2) * P], in_=ob[:])
 
@@ -364,11 +372,13 @@ def tile_fmmlayer_t_kernel(tc, x, freq, phase_shift, weight, out):
                 nc.tensor.matmul(out=wp[:], lhsT=pe_in[:, 0:P], rhs=pe_in[:], start=True, stop=True)
 
         H = -1
-        warm_pe(W0, H)
-        left(0, 0, 4, H)("s")
+        warm_pe(6, H)
+        left(0, 0, 2, H)("s")
         e00 = wt(0, 0, H)
         e00("v")
         a = [wmm(0, 0, 0, ol, H) for ol in range(2)]
+        l2 = left(0, 2, 4, H)
+        l2("v")
         e01 = wt(0, 1, H)
         e01("v")
         a += [wmm(0, 0, 1, ol, H) for ol in range(2)]
@@ -381,6 +391,7 @@ def tile_fmmlayer_t_kernel(tc, x, freq, phase_shift, weight, out):
         for f in a:
             f()
         lb("s")
+        warm_pe(2, H)
         e10 = wt(1, 0, H)
         e10("v")
         e11 = wt(1, 1, H)
@@ -388,6 +399,8 @@ def tile_fmmlayer_t_kernel(tc, x, freq, phase_shift, weight, out):
         wq(0, 0, 0)
         wq(0, 0, 1)
         for s in range(4):
+            if s == 2:
+                warm_pe(2, H)
             ex = xT(s, H)
             ex("s")
         mod(0, 1, 0)
@@ -442,49 +455,64 @@ def tile_fmmlayer_t_kernel(tc, x, freq, phase_shift, weight, out):
                 else:
                     later_dve.append(lambda: xqs.append(lambda: xq(c, sub % 2)))
 
-        pend.append(lambda: (mod(0, 2, 0), pend.append(lambda: wq(0, 2, 0))))
-        pend.append(lambda: (mod(0, 2, 1), pend.append(lambda: wq(0, 2, 1))))
         for g in range(2):
-            e3 = wt(3, g, 0)
-            later_dve.append(lambda e3=e3: e3("v"))
-        for ol in range(2):
-            w_unit(0, 3, 0, ol, 0)
+            mod(0, 2, g)
+            pend.append(lambda g=g: wq(0, 2, g))
         w_list = []
         for oq in range(4):
             for g in range(2):
                 for ol in range(2):
                     w_list.append(lambda i, oq=oq, g=g, ol=ol: w_unit(1, oq, g, ol, i))
 
+        def span(f, i):
+            return range(max(f(i - 1) + 1, 0), min(f(i), NPAIR - 1) + 1)
+
+        def r_at(i):
+            return span(lambda j: j - (D_R if j < CU else D_R - 1), i)
+
+        def out_at(i):
+            return span(lambda j: j - (D_T if j < CU + 1 else D_T - 1), i)
+
         for i in range(NPAIR + D_T):
             if i < NPAIR:
                 s_mx(i)
+            if i == 0:
+                s_u(0, False)
+                for g in range(2):
+                    e3 = wt(3, g, 0)
+                    later_dve.append(lambda e3=e3: e3("v"))
+                for ol in range(2):
+                    w_unit(0, 3, 0, ol, 0)
             for f in take(later_act):
                 f()
-            if i < NPAIR:
+            if 0 < i < NPAIR:
                 s_u(i, False)
             for f in take(xqs):
                 f()
             if 0 <= i - D_K < NPAIR:
                 s_k(i - D_K)
-            if 0 <= i - D_R < NPAIR:
-                s_r(i - D_R)
+            for n in r_at(i):
+                s_r(n)
             if i < NPAIR:
                 s_u(i, True)
             for f in take(later_dve):
                 f()
             for f in take(pend):
                 f()
-            if 0 <= i - D_T < NPAIR:
-                s_out(i - D_T, i)
             if i == 0:
                 for ol in range(2):
                     w_unit(0, 3, 1, ol, i)
                 lf1 = left(1, 0, 8, i)
                 later_act.append(lambda: lf1("s"))
                 x_unit(i)
-            elif i <= 16:
-                w_list[i - 1](i)
-            if i in (1, 2) or (i % 2 == 0 and 4 <= i < 18):
-                x_unit(i)
-            if i > 0:
-                x_unit(i)
+                continue
+            nx = 2 if i in (1, 2) or (i % XE == 0 and 4 <= i < 18) else 1
+            for what in ORDER2 if nx == 2 else ORDER1:
+                if what == "o":
+                    for n in out_at(i):
+                        s_out(n, i)
+                elif what == "w":
+                    if i <= 16:
+                        w_list[i - 1](i)
+                else:
+                    x_unit(i)

@@ -22,7 +22,7 @@ NCH = B * (ROWS // TQ)
 NPAIR = NCH * 4
 TWO_PI = 2.0 * math.pi
 
-D_K, D_R, D_T = 1, 2, 3
+D_K, D_R, D_T = 2, 3, 4
 W_END = 20
 X_END = 20
 U_DVE_FROM = 20
@@ -31,8 +31,11 @@ X_DVE_A = 20
 HALF_LAST = 2
 ORDER1 = "oxw"
 ORDER2 = "oxwx"
-XE = 2
-CU = 30
+CK = 29
+CR1 = 29
+CR2 = 30
+CT1 = 30
+CT2 = 31
 X_MOD = 2
 X_S_TO = 3
 
@@ -57,10 +60,10 @@ def tile_fmmlayer_t_kernel(tc, x, freq, phase_shift, weight, out):
         make_identity(nc, ident_b[:])
         ident_f = keep.tile([P, P], F32, name="ident_f")
         make_identity(nc, ident_f[:])
+        pe_in = keep.tile([P, 256], BF16, name="pe_in")
+        nc.vector.memset(pe_in[:], 0.0)
         psz = keep.tile([P, P], BF16, name="psz")
         nc.vector.memset(psz[:], 0.0)
-        pe_in = keep.tile([P, 512], BF16, name="pe_in")
-        nc.vector.memset(pe_in[:], 0.0)
         warm_in = keep.tile([P, 1], F32, name="warm_in")
         nc.vector.memset(warm_in[:], 0.0)
         warm_out = keep.tile([P, 1], F32, name="warm_out")
@@ -302,7 +305,7 @@ def tile_fmmlayer_t_kernel(tc, x, freq, phase_shift, weight, out):
                         stop=(g == 1),
                     )
                 ys[(i, ol)] = py
-            u_t = st4.tile([P, 2, 512], F32, name="u_t", tag="u")
+            u_t = st4.tile([P, 2, 512], F32, name="u_t", tag="u", bufs=5)
             us[i] = u_t
 
         def s_u(i, on_dve):
@@ -339,7 +342,7 @@ def tile_fmmlayer_t_kernel(tc, x, freq, phase_shift, weight, out):
                 nc.vector.tensor_copy(out=k_t[:, h, :], in_=us[i][:, h, :])
 
         def s_r(i):
-            r_t = st3.tile([P, 2, 512], F32, name="r_t", tag="r")
+            r_t = st3.tile([P, 2, 512], F32, name="r_t", tag="r", bufs=4)
             rs[i] = r_t
             for h in halves(i):
                 nc.vector.tensor_tensor(out=r_t[:, h, :], in0=us[i][:, h, :], in1=ks[i][:, h, :], op=ALU.subtract)
@@ -367,12 +370,12 @@ def tile_fmmlayer_t_kernel(tc, x, freq, phase_shift, weight, out):
                 nc.sync.dma_start(out=oview[:, :, 2 * pr * P : (2 * pr + 2) * P], in_=ob[:])
 
         def warm_pe(n, i):
-            wp = bank("x", i, [P, 512], F32)
+            wp = bank("x", i, [P, 256], F32)
             for m in range(n):
                 nc.tensor.matmul(out=wp[:], lhsT=pe_in[:, 0:P], rhs=pe_in[:], start=True, stop=True)
 
         H = -1
-        warm_pe(6, H)
+        warm_pe(10, H)
         left(0, 0, 2, H)("s")
         e00 = wt(0, 0, H)
         e00("v")
@@ -391,7 +394,7 @@ def tile_fmmlayer_t_kernel(tc, x, freq, phase_shift, weight, out):
         for f in a:
             f()
         lb("s")
-        warm_pe(2, H)
+        warm_pe(4, H)
         e10 = wt(1, 0, H)
         e10("v")
         e11 = wt(1, 1, H)
@@ -400,7 +403,7 @@ def tile_fmmlayer_t_kernel(tc, x, freq, phase_shift, weight, out):
         wq(0, 0, 1)
         for s in range(4):
             if s == 2:
-                warm_pe(2, H)
+                warm_pe(4, H)
             ex = xT(s, H)
             ex("s")
         mod(0, 1, 0)
@@ -467,30 +470,33 @@ def tile_fmmlayer_t_kernel(tc, x, freq, phase_shift, weight, out):
         def span(f, i):
             return range(max(f(i - 1) + 1, 0), min(f(i), NPAIR - 1) + 1)
 
+        def k_at(i):
+            return span(lambda j: j - (D_K if j < CK else 1), i)
+
         def r_at(i):
-            return span(lambda j: j - (D_R if j < CU else D_R - 1), i)
+            return span(lambda j: j - (D_R if j < CR1 else D_R - 1 if j < CR2 else D_R - 2), i)
 
         def out_at(i):
-            return span(lambda j: j - (D_T if j < CU + 1 else D_T - 1), i)
+            return span(lambda j: j - (D_T if j < CT1 else D_T - 1 if j < CT2 else D_T - 2), i)
 
         for i in range(NPAIR + D_T):
             if i < NPAIR:
                 s_mx(i)
             if i == 0:
                 s_u(0, False)
+                for ol in range(2):
+                    w_unit(0, 3, 0, ol, 0)
                 for g in range(2):
                     e3 = wt(3, g, 0)
                     later_dve.append(lambda e3=e3: e3("v"))
-                for ol in range(2):
-                    w_unit(0, 3, 0, ol, 0)
             for f in take(later_act):
                 f()
             if 0 < i < NPAIR:
                 s_u(i, False)
             for f in take(xqs):
                 f()
-            if 0 <= i - D_K < NPAIR:
-                s_k(i - D_K)
+            for n in k_at(i):
+                s_k(n)
             for n in r_at(i):
                 s_r(n)
             if i < NPAIR:
@@ -500,13 +506,13 @@ def tile_fmmlayer_t_kernel(tc, x, freq, phase_shift, weight, out):
             for f in take(pend):
                 f()
             if i == 0:
-                for ol in range(2):
-                    w_unit(0, 3, 1, ol, i)
                 lf1 = left(1, 0, 8, i)
                 later_act.append(lambda: lf1("s"))
                 x_unit(i)
+                for ol in range(2):
+                    w_unit(0, 3, 1, ol, i)
                 continue
-            nx = 2 if i in (1, 2) or (i % XE == 0 and 4 <= i < 18) else 1
+            nx = 2 if i in (1, 2) or (i % 2 == 0 and 4 <= i < 18) else 1
             for what in ORDER2 if nx == 2 else ORDER1:
                 if what == "o":
                     for n in out_at(i):

import math
from contextlib import ExitStack

import concourse.mybir as mybir
from concourse.masks import make_identity

F32 = mybir.dt.float32
BF16 = mybir.dt.bfloat16
I32 = mybir.dt.int32
U32 = mybir.dt.uint32
U8 = mybir.dt.uint8
FP8X4 = mybir.dt.float8_e4m3fn_x4
ACT = mybir.ActivationFunctionType
ALU = mybir.AluOpType

P = 128
B, N, CI, CO, R = 2, 2048, 1024, 1024, 128
FLOPS = 2 * B * N * CI * CO + 2 * B * CO * CI * R
ROWS = N // P
TQ = 4
NCH = B * (ROWS // TQ)
NPAIR = NCH * 4
TWO_PI = 2.0 * math.pi

D_K, D_R, D_T = 2, 3, 4
W_END = 20
X_END = 20
U_DVE_FROM = 20
U_MOD = 2
X_DVE_A = 20
HALF_LAST = 2
ORDER1 = "oxw"
ORDER2 = "oxwx"
CK = 29
CR1 = 29
CR2 = 30
CT1 = 30
CT2 = 31
X_MOD = 2
X_S_TO = 3


def take(queue):
    items = list(queue)
    queue[:] = []
    return items


def tile_fmmlayer_t_kernel(tc, x, freq, phase_shift, weight, out):
    nc = tc.nc
    with ExitStack() as ctx:
        keep = ctx.enter_context(tc.tile_pool(name="keep", bufs=1))
        xs_pool = ctx.enter_context(tc.tile_pool(name="xs", bufs=4))
        st3 = ctx.enter_context(tc.tile_pool(name="st3", bufs=3))
        st4 = ctx.enter_context(tc.tile_pool(name="st4", bufs=4))
        psum = ctx.enter_context(tc.psum_pool(name="psum", bufs=1))
        ctx.enter_context(tc.manual_schedule())

        ident_b = keep.tile([P, P], BF16, name="ident_b")
        make_identity(nc, ident_b[:])
        ident_f = keep.tile([P, P], F32, name="ident_f")
        make_identity(nc, ident_f[:])
        pe_in = keep.tile([P, 256], BF16, name="pe_in")
        nc.vector.memset(pe_in[:], 0.0)
        psz = keep.tile([P, P], BF16, name="psz")
        nc.vector.memset(psz[:], 0.0)
        warm_in = keep.tile([P, 1], F32, name="warm_in")
        nc.vector.memset(warm_in[:], 0.0)
        warm_out = keep.tile([P, 1], F32, name="warm_out")
        nc.scalar.activation(out=warm_out[:], in_=warm_in[:], func=ACT.Silu)

        lf = []
        rt = []
        wn = []
        for b in range(B):
            lf.append(keep.tile([P, 8, R], BF16, name="lf%d" % b))
            rt.append(keep.tile([P, CI], BF16, name="rt%d" % b))
        for k in range(4):
            wn.append([keep.tile([P, 2, CI // 2], BF16, name="wn%d_%d" % (k, g)) for g in range(2)])
        wview = weight.rearrange("(t p) i -> p t i", p=P)

        def load_left(b, t0, t1):
            nc.sync.dma_start(
                out=lf[b][:, t0:t1, :],
                in_=freq[b, t0 * P * R : t1 * P * R].rearrange("(t p r) -> p t r", t=t1 - t0, p=P),
            )

        def load_right(b, g=None):
            i0, i1 = (0, CI) if g is None else (512 * g, 512 * g + 512)
            nc.sync.dma_start(
                out=rt[b][:, i0:i1], in_=freq[b, CO * R : CO * R + R * CI].rearrange("(r i) -> r i", r=R)[:, i0:i1]
            )

        def load_w(k, g):
            nc.sync.dma_start(out=wn[k][g][:], in_=wview[:, 2 * k : 2 * k + 2, 512 * g : 512 * (g + 1)])

        xs = {}

        def load_x(c, parts=1):
            b, q = divmod(c, 4)
            xs_t = xs_pool.tile([P, TQ, CI], BF16, name="xs_t", tag="xs")
            w = TQ // parts
            for h in range(parts):
                t0 = TQ * q + w * h
                nc.sync.dma_start(
                    out=xs_t[:, w * h : w * h + w, :],
                    in_=x[b].rearrange("(j s) i -> j s i", s=ROWS)[:, t0 : t0 + w, :],
                )
            xs[c] = xs_t

        load_left(0, 0, 2)
        load_right(0, 0)
        load_w(0, 0)
        load_left(0, 2, 4)
        load_right(0, 1)
        load_w(0, 1)
        load_left(0, 4, 8)
        load_w(1, 0)
        load_w(1, 1)
        load_x(0, 2)
        load_w(2, 0)
        load_w(2, 1)
        nc.sync.dma_start(out=psz[0:32, :], in_=phase_shift.rearrange("b (r c) -> (b r) c", c=P))
        load_w(3, 0)
        load_w(3, 1)
        load_x(1)
        load_left(1, 0, 8)
        load_right(1)
        load_x(2)
        load_x(3)

        turn = {"head": 0, "y": 0, "t": 0, "w": 0, "x": 0}

        def bank(role, i, shape, dtype):
            if i < 0:
                banks, role = (0, 1, 2, 3, 4, 5, 6, 7), "head"
            elif role == "y":
                banks = (0, 1, 4, 5) if i >= W_END else (0, 1)
            elif role == "t":
                banks = (2, 3, 6, 7) if i >= X_END else (2, 3)
            elif role == "w":
                banks = (4, 5)
            else:
                banks = (6, 7)
            n = turn[role]
            turn[role] += 1
            ps = psum.tile(shape, dtype, name="ps", tag="bank%d" % banks[n % len(banks)])
            return ps

        fs2 = keep.tile([P, B, 8], F32, name="fs2")
        ph2 = keep.tile([P, B, 8], F32, name="ph2")

        def phase(i):
            pps = bank("x", i, [P, P], BF16)
            nc.tensor.transpose(pps[:], psz[:], ident_b[:])

            def leave():
                psv = pps[:, 0:32].rearrange("p (b h o) -> p b h o", b=B, h=2)
                nc.vector.tensor_scalar(
                    out=fs2[:], in0=psv[:, :, 0, :], scalar1=0.5 / TWO_PI, scalar2=None, op0=ALU.mult
                )
                nc.vector.tensor_scalar(
                    out=ph2[:], in0=psv[:, :, 1, :], scalar1=-30.0, scalar2=1.0 / (15.0 * TWO_PI), op0=ALU.add, op1=ALU.mult
                )

            return leave

        lT = []
        wc = []
        wsc = []
        for b in range(B):
            lT.append(keep.tile([P, CO], BF16, name="lT%d" % b))
            wc.append(keep.tile([P, 2, CO], U32, name="wc%d" % b, align_bytes=64))
            wsc.append(keep.tile([P, 2, CO], U8, name="wsc%d" % b, align_bytes=64))
        wTh = keep.tile([P, 2, CO, 4], BF16, name="wTh")
        wThf = wTh[:].bitcast(F32)

        def copy_on(engine, dst, src):
            if engine == "v":
                nc.vector.tensor_copy(out=dst, in_=src)
            else:
                nc.scalar.copy(out=dst, in_=src)

        def left(b, t0, t1, i):
            plf = bank("x", i, [P, 8, P], BF16)
            for t in range(t0, t1):
                nc.tensor.transpose(plf[:, t - t0, :], lf[b][:, t, :], ident_b[:])
            return lambda e: copy_on(
                e, lT[b][:, t0 * P : t1 * P], plf[:, 0 : t1 - t0, :].rearrange("p t o -> p (t o)")
            )

        def wt(k, g, i):
            wnf = wn[k][g][:].bitcast(F32)
            pw = bank("t", i, [P, 2, 256], F32)
            for u in range(2):
                for ol in range(2):
                    nc.tensor.transpose(pw[:, u, ol * P : (ol + 1) * P], wnf[:, ol, u:256:2], ident_f[:])
            return lambda e: copy_on(e, wThf[:, g, 256 * k : 256 * k + 256, :], pw[:].rearrange("p u o -> p o u"))

        ths = {}
        gws = {}

        def wmm(b, oq, g, ol, i):
            if ol == 0:
                th = st3.tile([P, 256, 4], F32, name="th", tag="th")
                ths[(b, oq, g)] = th
            ot = 2 * oq + ol
            rtv = rt[b][:].rearrange("r (g p u e) -> r g u e p", g=2, u=2, p=P, e=2)
            pm = bank("w", i, [P, 4, P], F32)
            for u in range(2):
                for e in range(2):
                    nc.tensor.matmul(
                        out=pm[:, 2 * u + e, :],
                        lhsT=rtv[:, g, u, e, :],
                        rhs=lT[b][:, ot * P : (ot + 1) * P],
                        start=True,
                        stop=True,
                    )
            return lambda: nc.scalar.activation(
                out=ths[(b, oq, g)][:, ol * P : (ol + 1) * P, :],
                in_=pm[:].rearrange("p t o -> p o t"),
                func=ACT.Tanh,
                scale=0.5 / math.sqrt(R),
            )

        def mod(b, oq, g):
            gw = st3.tile([P, 256, 4], BF16, name="gw", tag="gw", align_bytes=64)
            gws[(b, oq, g)] = gw
            nc.vector.scalar_tensor_tensor(
                out=gw[:].rearrange("p o t -> p (o t)"),
                in0=ths[(b, oq, g)][:].rearrange("p o t -> p (o t)"),
                scalar=2.0,
                in1=wTh[:, g, 256 * oq : 256 * oq + 256, :].rearrange("p o t -> p (o t)"),
                op0=ALU.add,
                op1=ALU.mult,
            )

        def wq(b, oq, g):
            nc.vector.quantize_mx(
                out=wc[b][:, g, 256 * oq : 256 * oq + 256].bitcast(FP8X4),
                scales=wsc[b][:, g, 256 * oq : 256 * oq + 256],
                in_=gws[(b, oq, g)][:].rearrange("p o t -> p (o t)"),
            )

        xc = {}
        xsc = {}
        gx = {}

        def xq(c, g):
            nc.vector.quantize_mx(
                out=xc[c][:, g, :].bitcast(FP8X4),
                scales=xsc[c][:, g, :],
                in_=gx[(c, g)][:].rearrange("p n t -> p (n t)"),
            )

        def xT(s, i):
            c, sub = divmod(s, 4)
            tp, g = divmod(sub, 2)
            if sub == 0:
                xc_t = st3.tile([P, 2, 512], U32, name="xc_t", tag="xc", bufs=5, align_bytes=64)
                xsc_t = st3.tile([P, 2, 512], U8, name="xsc_t", tag="xsc", bufs=5, align_bytes=64)
                xc[c] = xc_t
                xsc[c] = xsc_t
            if tp == 0:
                gx_t = st4.tile([P, 512, 4], BF16, name="gx_t", tag="gx", align_bytes=64)
                gx[(c, g)] = gx_t
            xf = xs[c][:].bitcast(F32)
            px = bank("x", i, [P, 2, 256], F32)
            for u in range(2):
                for tl in range(2):
                    nc.tensor.transpose(
                        px[:, u, tl * P : (tl + 1) * P],
                        xf[:, 2 * tp + tl, 256 * g + u : 256 * (g + 1) : 2],
                        ident_f[:],
                    )
            if sub == 3 and c + 4 < NCH:
                load_x(c + 4)
            dst = gx[(c, g)][:].bitcast(F32)[:, 256 * tp : 256 * tp + 256, :]
            src = px[:].rearrange("p u n -> p n u")
            return lambda e: copy_on(e, dst, src)

        ys = {}
        us = {}
        ks = {}
        rs = {}

        def where(i):
            c, pr = divmod(i, 4)
            b, q = divmod(c, 4)
            return b, q, c, pr

        def s_mx(i):
            b, q, c, pr = where(i)
            for ol in range(2):
                ot = 2 * pr + ol
                py = bank("y", i, [P, 512], F32)
                for g in range(2):
                    nc.tensor.matmul_mx(
                        out=py[:],
                        lhsT=wc[b][:, g, ot * P : (ot + 1) * P].bitcast(FP8X4),
                        lhsT_scale=wsc[b][:, g, ot * P : (ot + 1) * P],
                        rhs=xc[c][:, g, :].bitcast(FP8X4),
                        rhs_scale=xsc[c][:, g, :],
                        start=(g == 0),
                        stop=(g == 1),
                    )
                ys[(i, ol)] = py
            u_t = st4.tile([P, 2, 512], F32, name="u_t", tag="u", bufs=5)
            us[i] = u_t

        def s_u(i, on_dve):
            b, q, c, pr = where(i)
            for ol in range(2):
                ot = 2 * pr + ol
                if (i >= U_DVE_FROM and i % U_MOD == 0 and ol == 1) != on_dve:
                    continue
                if on_dve:
                    nc.vector.tensor_scalar(
                        out=us[i][:, ol, :],
                        in0=ys[(i, ol)][:],
                        scalar1=fs2[:, b, ot : ot + 1],
                        scalar2=ph2[:, b, ot : ot + 1],
                        op0=ALU.mult,
                        op1=ALU.add,
                    )
                else:
                    nc.scalar.activation(
                        out=us[i][:, ol, :],
                        in_=ys[(i, ol)][:],
                        func=ACT.Identity,
                        scale=fs2[:, b, ot : ot + 1],
                        bias=ph2[:, b, ot : ot + 1],
                    )

        def halves(i):
            return [slice(0, 1), slice(1, 2)] if i >= NPAIR - HALF_LAST else [slice(0, 2)]

        def s_k(i):
            k_t = st3.tile([P, 2, 512], I32, name="k_t", tag="k")
            ks[i] = k_t
            for h in halves(i):
                nc.vector.tensor_copy(out=k_t[:, h, :], in_=us[i][:, h, :])

        def s_r(i):
            r_t = st3.tile([P, 2, 512], F32, name="r_t", tag="r", bufs=4)
            rs[i] = r_t
            for h in halves(i):
                nc.vector.tensor_tensor(out=r_t[:, h, :], in0=us[i][:, h, :], in1=ks[i][:, h, :], op=ALU.subtract)

        def s_out(i, j):
            b, q, c, pr = where(i)
            pts = []
            for ol in range(2):
                pt = bank("t", j, [P, TQ, P], F32)
                for t in range(TQ):
                    nc.tensor.transpose(pt[:, t, :], rs[i][:, ol, t * P : (t + 1) * P], ident_f[:])
                pts.append(pt)
            ob = st4.tile([P, TQ, 2 * P], F32, name="ob", tag="ob")
            oview = out[b].rearrange("(j s) o -> j s o", s=ROWS)[:, TQ * q : TQ * q + TQ, :]
            for ol in range(2):
                cuts = [slice(0, 2), slice(2, 4)] if i == NPAIR - 1 else [slice(0, 4)]
                for ts in cuts:
                    nc.scalar.activation(
                        out=ob[:, ts, ol * P : (ol + 1) * P], in_=pts[ol][:, ts, :], func=ACT.Sin, scale=TWO_PI
                    )
                    if i == NPAIR - 1:
                        o0 = (2 * pr + ol) * P
                        nc.sync.dma_start(out=oview[:, ts, o0 : o0 + P], in_=ob[:, ts, ol * P : (ol + 1) * P])
            if i < NPAIR - 1:
                nc.sync.dma_start(out=oview[:, :, 2 * pr * P : (2 * pr + 2) * P], in_=ob[:])

        def warm_pe(n, i):
            wp = bank("x", i, [P, 256], F32)
            for m in range(n):
                nc.tensor.matmul(out=wp[:], lhsT=pe_in[:, 0:P], rhs=pe_in[:], start=True, stop=True)

        H = -1
        warm_pe(10, H)
        left(0, 0, 2, H)("s")
        e00 = wt(0, 0, H)
        e00("v")
        a = [wmm(0, 0, 0, ol, H) for ol in range(2)]
        l2 = left(0, 2, 4, H)
        l2("v")
        e01 = wt(0, 1, H)
        e01("v")
        a += [wmm(0, 0, 1, ol, H) for ol in range(2)]
        for f in a:
            f()
        mod(0, 0, 0)
        a = [wmm(0, 1, g, ol, H) for g in range(2) for ol in range(2)]
        mod(0, 0, 1)
        lb = left(0, 4, 8, H)
        for f in a:
            f()
        lb("s")
        warm_pe(4, H)
        e10 = wt(1, 0, H)
        e10("v")
        e11 = wt(1, 1, H)
        e11("v")
        wq(0, 0, 0)
        wq(0, 0, 1)
        for s in range(4):
            if s == 2:
                warm_pe(4, H)
            ex = xT(s, H)
            ex("s")
        mod(0, 1, 0)
        a = [wmm(0, 2, 0, ol, H) for ol in range(2)]
        for f in a:
            f()
        mod(0, 1, 1)
        a = [wmm(0, 2, 1, ol, H) for ol in range(2)]
        for f in a:
            f()
        xq(0, 0)
        xq(0, 1)
        ph = phase(H)
        ph()
        wq(0, 1, 0)
        wq(0, 1, 1)
        e20 = wt(2, 0, H)
        e20("s")
        e21 = wt(2, 1, H)
        e21("s")

        later_act = []
        later_dve = []
        pend = []
        xqs = []
        x_pos = {"s": 4}

        def w_unit(b, oq, g, ol, i):
            f = wmm(b, oq, g, ol, i)

            def go():
                f()
                if ol == 1:
                    pend.append(lambda: (mod(b, oq, g), pend.append(lambda: wq(b, oq, g))))

            later_act.append(go)

        def x_unit(i):
            s = x_pos["s"]
            if s >= 4 * NCH:
                return
            x_pos["s"] += 1
            c, sub = divmod(s, 4)
            ex = xT(s, i)
            if i < X_S_TO or (i < X_DVE_A and s % X_MOD == 0):
                later_act.append(lambda: ex("s"))
            else:
                later_dve.append(lambda: ex("v"))
            if sub >= 2:
                if i < W_END:
                    later_dve.append(lambda: pend.append(lambda: xq(c, sub % 2)))
                else:
                    later_dve.append(lambda: xqs.append(lambda: xq(c, sub % 2)))

        for g in range(2):
            mod(0, 2, g)
            pend.append(lambda g=g: wq(0, 2, g))
        w_list = []
        for oq in range(4):
            for g in range(2):
                for ol in range(2):
                    w_list.append(lambda i, oq=oq, g=g, ol=ol: w_unit(1, oq, g, ol, i))

        def span(f, i):
            return range(max(f(i - 1) + 1, 0), min(f(i), NPAIR - 1) + 1)

        def k_at(i):
            return span(lambda j: j - (D_K if j < CK else 1), i)

        def r_at(i):
            return span(lambda j: j - (D_R if j < CR1 else D_R - 1 if j < CR2 else D_R - 2), i)

        def out_at(i):
            return span(lambda j: j - (D_T if j < CT1 else D_T - 1 if j < CT2 else D_T - 2), i)

        for i in range(NPAIR + D_T):
            if i < NPAIR:
                s_mx(i)
            if i == 0:
                s_u(0, False)
                for ol in range(2):
                    w_unit(0, 3, 0, ol, 0)
                for g in range(2):
                    e3 = wt(3, g, 0)
                    later_dve.append(lambda e3=e3: e3("v"))
            for f in take(later_act):
                f()
            if 0 < i < NPAIR:
                s_u(i, False)
            for f in take(xqs):
                f()
            for n in k_at(i):
                s_k(n)
            for n in r_at(i):
                s_r(n)
            if i < NPAIR:
                s_u(i, True)
            for f in take(later_dve):
                f()
            for f in take(pend):
                f()
            if i == 0:
                lf1 = left(1, 0, 8, i)
                later_act.append(lambda: lf1("s"))
                x_unit(i)
                for ol in range(2):
                    w_unit(0, 3, 1, ol, i)
                continue
            nx = 2 if i in (1, 2) or (i % 2 == 0 and 4 <= i < 18) else 1
            for what in ORDER2 if nx == 2 else ORDER1:
                if what == "o":
                    for n in out_at(i):
                        s_out(n, i)
                elif what == "w":
                    if i <= 16:
                        w_list[i - 1](i)
                else:
                    x_unit(i)
